import numpy as np
import ml_dtypes


BF16 = ml_dtypes.bfloat16


def bf(x):
    return np.asarray(x, np.float32).astype(BF16)


def f64(x):
    return np.asarray(x).astype(np.float64)


E2M1 = np.array([0.0, 0.5, 1.0, 1.5, 2.0, 3.0, 4.0, 6.0, -0.0, -0.5, -1.0, -1.5, -2.0, -3.0, -4.0, -6.0])


def pack_weight(w, fmt):
    k, n = w.shape
    w = f64(bf(w)).reshape(k // 32, 32, n)
    amax = np.abs(w).max(1)
    if fmt == "e4m3":
        byte = np.frexp(amax)[1] - 1 + 127 - 7
    else:
        mant, ex = np.frexp(amax / 6.0)
        byte = np.where(mant > 0.5, ex, ex - 1) + 127
    byte = np.clip(np.where(amax > 0, byte, 1), 1, 254)
    scaled = (w * np.exp2(127.0 - byte)[:, None, :]).reshape(k, n).astype(np.float32)
    by_word = np.ascontiguousarray(scaled.reshape(k // 512, 128, 4, n).transpose(0, 1, 3, 2))
    if fmt == "e4m3":
        words = by_word.astype(ml_dtypes.float8_e4m3fn).view(np.uint8)
    else:
        c = by_word.astype(ml_dtypes.float4_e2m1fn).view(np.uint8) & 0xF
        words = c[..., 0::2] | (c[..., 1::2] << 4)
    return np.ascontiguousarray(words), np.ascontiguousarray(byte.astype(np.uint8).reshape(k // 512, 16, n))


def unpack_weight(words, scales, fmt):
    g, p, n, _ = words.shape
    if fmt == "e4m3":
        vals = np.ascontiguousarray(words).view(ml_dtypes.float8_e4m3fn).astype(np.float64)
    else:
        nib = np.empty((g, p, n, 4), np.uint8)
        nib[..., 0::2] = words & 0xF
        nib[..., 1::2] = words >> 4
        vals = E2M1[nib]
    vals = vals * np.repeat(np.exp2(scales.astype(np.float64) - 127.0), 8, axis=1)[..., None]
    return vals.transpose(0, 1, 3, 2).reshape(g * 512, n)

def pack4(w):
    words, scales = pack_weight(w, "e2m1")
    return words.reshape(words.shape[0], 128, -1), scales


def unpack4(words, scales):
    return unpack_weight(words.reshape(words.shape[0], 128, -1, 2), scales, "e2m1")


def kspread(k):
    return np.exp2(np.repeat(np.random.randint(-6, 7, k // 32), 32).astype(np.float64))


B, T, KA, KT, DIM, NH, HD, E = 2, 256, 256, 256, 3072, 8, 128, 8
ROPE_BASE = 10000.0


def rope_cos_sin(L, hd):
    inv_freq = 1.0 / (ROPE_BASE ** (f64(np.arange(0, hd, 2)) / hd))
    freqs = f64(np.arange(L))[:, None] * inv_freq[None, :]
    emb = np.concatenate([freqs, freqs], axis=-1)
    return np.cos(emb), np.sin(emb)


def rotate_half(x):
    x1 = x[..., 0::2]
    x2 = x[..., 1::2]
    return np.stack((-x2, x1), axis=-1).reshape(x.shape)


def rope(t, cos, sin):
    return t * cos[None, None] + rotate_half(t) * sin[None, None]


def heads(t):
    return t.reshape(B, -1, NH, HD).transpose(0, 2, 1, 3)


def setup_inputs():
    s = kspread(DIM)
    c = 1.2 / np.sqrt(DIM)
    x = np.random.standard_normal((B, T, DIM)) * s
    x_words, x_scales = pack4(x.reshape(B * T, DIM).T)
    qa_words, qa_scales = pack4((np.random.standard_normal((NH * HD, DIM)) * c / s[None, :]).T)
    b_qa = bf(np.random.standard_normal(NH * HD) * 0.3)
    qt_words, qt_scales = pack4((np.random.standard_normal((NH * HD, DIM)) * c / s[None, :]).T)
    b_qt = bf(np.random.standard_normal(NH * HD) * 0.3)
    return {"x_words": x_words,
            "x_scales": x_scales,
            "W_qa_words": qa_words,
            "W_qa_scales": qa_scales,
            "b_qa": b_qa,
            "W_qt_words": qt_words,
            "W_qt_scales": qt_scales,
            "b_qt": b_qt}


def reference(x_words, x_scales, W_qa_words, W_qa_scales, b_qa, W_qt_words, W_qt_scales, b_qt):
    xq = unpack4(x_words, x_scales).T.reshape(B, T, DIM)
    q_a = heads((xq @ unpack4(W_qa_words, W_qa_scales)) + f64(b_qa))
    q_t = heads((xq @ unpack4(W_qt_words, W_qt_scales)) + f64(b_qt))
    cos_m, sin_m = rope_cos_sin(T, HD)
    return rope(q_a, cos_m, sin_m), rope(q_t, cos_m, sin_m)

@@ -1,0 +1,245 @@
+import math
+from contextlib import ExitStack
+
+import concourse.mybir as mybir
+from concourse.masks import make_identity
+
+F32 = mybir.dt.float32
+BF16 = mybir.dt.bfloat16
+I32 = mybir.dt.int32
+U8 = mybir.dt.uint8
+FP4X4 = mybir.dt.float4_e2m1fn_x4
+ALU = mybir.AluOpType
+ACT = mybir.ActivationFunctionType
+
+P = 128
+PASSES = 6
+TOKENS = 512
+M_TILES = 4
+N_TILE = 512
+N_TILES = 4
+HEAD = 128
+HALF = 64
+WARM_UP = 12
+PAIRED_UNITS = 8
+GPSIMD_COSINE_UNITS = (3, 8)
+SBUF_TABLE_UNITS = 0
+
+FLOPS = 2 * 512 * 2048 * 3072
+
+RATIO = 10000.0 ** (-1.0 / 64.0)
+
+
+def tile_l1regressionmoeactionhead_pa_kernel(
+    tc, x_words, x_scales, W_qa_words, W_qa_scales, b_qa, W_qt_words, W_qt_scales, b_qt, out_0, out_1
+):
+    nc = tc.nc
+    w_words = (W_qa_words, W_qt_words)
+    w_scales = (W_qa_scales, W_qt_scales)
+    outs = (out_0, out_1)
+
+    with ExitStack() as ctx:
+        keep = ctx.enter_context(tc.tile_pool(name="keep", bufs=1))
+        work = ctx.enter_context(tc.tile_pool(name="work", bufs=3))
+        acc_pool = ctx.enter_context(tc.psum_pool(name="acc", bufs=7))
+        tab_pool = ctx.enter_context(tc.psum_pool(name="tab", bufs=1))
+        ctx.enter_context(tc.manual_schedule())
+
+        xw = [keep.tile([P, PASSES, 512], U8, name="xw%d" % h, align_bytes=64) for h in range(2)]
+        xs = keep.tile([P, PASSES, TOKENS], U8, name="xs", align_bytes=64)
+        w0 = [keep.tile([P, 3, 2 * N_TILE], U8, name="w0%d" % h, align_bytes=64) for h in range(2)]
+        ww = [None] + [keep.tile([P, PASSES, 2 * N_TILE], U8, name="ww%d" % n, align_bytes=64) for n in range(1, N_TILES)]
+        ws = [keep.tile([P, PASSES, N_TILE], U8, name="ws%d" % n, align_bytes=64) for n in range(N_TILES)]
+
+        def w_codes(n, g):
+            if n == 0:
+                return w0[g // 3][:, g % 3, :]
+            return ww[n][:, g, :]
+
+        brow = keep.tile([P, N_TILE], BF16, name="brow")
+        nc.vector.memset(brow[:], 0.0)
+        zero = keep.tile([P, P], BF16, name="zero")
+        nc.vector.memset(zero[:], 0.0)
+        nc.vector.memset(xs[:].bitcast(I32), 0)
+        turns = keep.tile([P, 2, HALF], F32, name="turns")
+        nc.gpsimd.iota(
+            turns[:, :, 0:1], pattern=[[-P, 2], [0, 1]], base=0, channel_multiplier=-1, allow_small_or_imprecise_dtypes=True
+        )
+        ident = keep.tile([P, P], F32, name="ident")
+        nc.vector.memset(ident[:], 0.0)
+        make_identity(nc, ident[:], nomemset=True)
+
+        def widen(w):
+            for k in (1, 2, 3):
+                factor = RATIO ** (k * w)
+                if (k * w) % 2 == 1:
+                    factor = -factor
+                nc.vector.tensor_scalar(
+                    out=turns[:, :, k * w : (k + 1) * w], in0=turns[:, :, 0:w], scalar1=factor, scalar2=None, op0=ALU.mult
+                )
+
+        widen(1)
+        nc.vector.memset(ws[0][:].bitcast(I32), 0)
+
+        def load_scales(planes, scales, c0, c1):
+            for q in range(4):
+                nc.sync.dma_start(
+                    out=planes[32 * q : 32 * q + 4, :, :].bitcast(I32),
+                    in_=scales[:, 4 * q : 4 * q + 4, c0:c1].rearrange("g r n -> r g n").bitcast(I32),
+                )
+
+        def load_codes(tile_ap, words, g0, g1, c0, c1):
+            nc.sync.dma_start(
+                out=tile_ap[:].bitcast(I32),
+                in_=words[g0:g1, :, c0:c1].rearrange("g p c -> p g c").bitcast(I32),
+            )
+
+        nc.scalar.dma_start(out=brow[0:2, :], in_=b_qa.rearrange("(o n) -> o n", o=2))
+        nc.scalar.dma_start(out=brow[2:4, :], in_=b_qt.rearrange("(o n) -> o n", o=2))
+        load_codes(xw[0], x_words, 0, PASSES, 0, 512)
+        load_codes(w0[0], w_words[0], 0, 3, 0, 2 * N_TILE)
+        load_scales(xs, x_scales, 0, TOKENS)
+        load_scales(ws[0], w_scales[0], 0, N_TILE)
+        load_codes(w0[1], w_words[0], 3, PASSES, 0, 2 * N_TILE)
+        load_codes(xw[1], x_words, 0, PASSES, 512, 1024)
+
+        warm = keep.tile([P, 1], F32, name="warm")
+        nc.scalar.activation(out=warm[:], in_=zero[:, 0:1], func=ACT.Sin)
+        ident_bf = keep.tile([P, P], BF16, name="ident_bf")
+        nc.scalar.copy(out=ident_bf[:], in_=ident[:])
+
+        junk = acc_pool.tile([P, P], F32, name="junk", tag="acc")
+        for i in range(WARM_UP):
+            nc.tensor.matmul(out=junk[:], lhsT=zero[:], rhs=zero[:], start=True, stop=True)
+
+        bias = keep.tile([P, 4 * N_TILE], F32, name="bias")
+
+        bias_ps = []
+        for n in range(N_TILES):
+            bp = acc_pool.tile([P, N_TILE], F32, name="bias_ps%d" % n, tag="acc")
+            nc.tensor.matmul(out=bp[:], lhsT=ident_bf[:, n : n + 1].to_broadcast([P, P]), rhs=brow[:], start=True, stop=True)
+            bias_ps.append(bp)
+        nc.scalar.copy(out=bias[:, 0:N_TILE], in_=bias_ps[0][:])
+
+        widen(4)
+        widen(16)
+        flat = turns[:].rearrange("p m j -> p (m j)")
+        whole = keep.tile([P, 2, 2 * HALF], I32, name="whole")
+        nc.vector.tensor_scalar(out=whole[:, 0, :], in0=flat, scalar1=1.0 / (2.0 * math.pi), scalar2=None, op0=ALU.mult)
+        nc.vector.tensor_scalar(
+            out=whole[:, 1, :], in0=flat, scalar1=1.0 / (2.0 * math.pi), scalar2=0.25, op0=ALU.mult, op1=ALU.add
+        )
+        frac = keep.tile([P, 2, 2 * HALF], F32, name="frac")
+        tab = keep.tile([P, 2, 2, HALF], F32, name="tab")
+        tab_ps = tab_pool.tile([P, 2, 2, HALF], F32, name="tab_ps")
+        for kind in range(2):
+            nc.vector.scalar_tensor_tensor(
+                out=frac[:, kind, :], in0=whole[:, kind, :], scalar=-2.0 * math.pi, in1=flat, op0=ALU.mult, op1=ALU.add
+            )
+        for kind in range(2):
+            nc.scalar.activation(
+                out=tab[:, kind, :, :].rearrange("p m j -> p (m j)"),
+                in_=frac[:, kind, :],
+                func=ACT.Sin,
+                bias=kind * math.pi / 2.0,
+            )
+            nc.tensor.matmul(
+                out=tab_ps[:, kind, :, :].rearrange("p m j -> p (m j)"),
+                lhsT=ident[:],
+                rhs=tab[:, kind, :, :].rearrange("p m j -> p (m j)"),
+                start=True,
+                stop=True,
+            )
+        for n in range(1, N_TILES):
+            nc.scalar.copy(out=bias[:, n * N_TILE : (n + 1) * N_TILE], in_=bias_ps[n][:])
+
+        for n in range(1, N_TILES):
+            nc.vector.memset(ws[n][:].bitcast(I32), 0)
+        for n in range(1, N_TILES):
+            c = n % 2
+            load_scales(ws[n], w_scales[n // 2], c * N_TILE, (c + 1) * N_TILE)
+            load_codes(ww[n], w_words[n // 2], 0, PASSES, c * 2 * N_TILE, (c + 1) * 2 * N_TILE)
+
+        units = [(n, m, 0, N_TILE) for n in range(N_TILES) for m in range(M_TILES)]
+        units = units[:-1] + [(N_TILES - 1, M_TILES - 1, 0, 256), (N_TILES - 1, M_TILES - 1, 256, 256)]
+        z_of = {}
+        block_of = {}
+
+        def block(k):
+            key = k // 2 if k < PAIRED_UNITS else PAIRED_UNITS + k
+            if key not in block_of:
+                width = 2 * N_TILE if k < PAIRED_UNITS else units[k][3]
+                kind = "2" if k < PAIRED_UNITS else "1"
+                block_of[key] = [
+                    work.tile([P, width], F32, name=nm + kind, tag=nm + kind, bufs=5) for nm in ("zc", "zs", "res")
+                ]
+            c0 = (k % 2) * N_TILE if k < PAIRED_UNITS else 0
+            return block_of[key], c0
+
+        def project(k):
+            n, m, c0, w = units[k]
+            acc = acc_pool.tile([P, w], F32, name="acc", tag="acc")
+            for g in range(PASSES):
+                nc.tensor.matmul_mx(
+                    out=acc[:],
+                    lhsT=xw[m // 2][:, g, 256 * (m % 2) : 256 * (m % 2 + 1)].bitcast(FP4X4),
+                    lhsT_scale=xs[:, g, P * m : P * (m + 1)],
+                    rhs=w_codes(n, g)[:, 2 * c0 : 2 * (c0 + w)].bitcast(FP4X4),
+                    rhs_scale=ws[n][:, g, c0 : c0 + w],
+                    start=(g == 0),
+                    stop=(g == PASSES - 1),
+                )
+            z = work.tile([P, w], F32, name="z", tag="z", bufs=6)
+            nc.vector.tensor_tensor(out=z[:], in0=acc[:], in1=bias[:, n * N_TILE + c0 : n * N_TILE + c0 + w], op=ALU.add)
+            z_of[k] = z
+
+        def times_cosine(k):
+            n, m, c0, w = units[k]
+            tiles, b0 = block(k)
+            on_gpsimd = k in GPSIMD_COSINE_UNITS
+            engine = nc.gpsimd if on_gpsimd else nc.vector
+            table = tab if (on_gpsimd or k < SBUF_TABLE_UNITS) else tab_ps
+            engine.tensor_tensor(
+                out=tiles[0][:, b0 : b0 + w].rearrange("p (c j) -> p c j", j=HALF),
+                in0=z_of[k][:].rearrange("p (c j) -> p c j", j=HALF),
+                in1=table[:, 1, m % 2, :].unsqueeze(1).to_broadcast([P, w // HALF, HALF]),
+                op=ALU.mult,
+            )
+
+        def times_sine(k):
+            n, m, c0, w = units[k]
+            tiles, b0 = block(k)
+            table = tab if k < SBUF_TABLE_UNITS else tab_ps
+            nc.vector.tensor_tensor(
+                out=tiles[1][:, b0 : b0 + w].rearrange("p (c i t) -> p c i t", i=HALF // 2, t=2),
+                in0=z_of[k][:].rearrange("p (c i t) -> p c i t", i=HALF // 2, t=2)[:, :, :, ::-1],
+                in1=table[:, 0, m % 2, :].rearrange("p (i t) -> p i t", t=2).unsqueeze(1).to_broadcast([P, w // HALF, HALF // 2, 2]),
+                op=ALU.mult,
+            )
+
+        def finish(ks, engine):
+            tiles, b0 = block(ks[0])
+            engine.tensor_tensor(out=tiles[2][:], in0=tiles[0][:], in1=tiles[1][:], op=ALU.add)
+            for k in ks:
+                n, m, c0, w = units[k]
+                tiles, b0 = block(k)
+                h0 = (n % 2) * 4 + c0 // HEAD
+                pt = m % 2
+                nc.scalar.dma_start(
+                    out=outs[n // 2][m // 2, h0 : h0 + w // HEAD, pt * P : (pt + 1) * P, :].rearrange("h p d -> p h d"),
+                    in_=tiles[2][:, b0 : b0 + w].rearrange("p (h d) -> p h d", d=HEAD),
+                )
+
+        last = len(units) - 1
+        for k in range(len(units)):
+            project(k)
+            if k > 0:
+                times_sine(k - 1)
+            times_cosine(k)
+            if k > 0:
+                if k - 1 >= PAIRED_UNITS:
+                    finish([k - 1], nc.gpsimd)
+                elif (k - 1) % 2 == 1:
+                    finish([k - 2, k - 1], nc.gpsimd)
+        times_sine(last)
+        finish([last], nc.vector)

@@ -21,9 +21,25 @@ N_TILES = 4
 HEAD = 128
 HALF = 64
 WARM_UP = 12
+WARM_N = 128
 PAIRED_UNITS = 8
 GPSIMD_COSINE_UNITS = (3, 8)
 SBUF_TABLE_UNITS = 0
+Q_ORDER = (0, 2, 1, 3)
+XW_GROUPS = ((0, 1), (1, 2), (2, 4),)
+XS_GROUPS = ((0, 2), (2, 4),)
+W0_SPLIT = (2, 2, 2,)
+HEAD_LOADS = ("xw0", "w0_0", "xs0", "ws0", "w0_1", "w0_2", "xw1",)
+HEAD_LOADS_2 = ("xs1", "xw2",)
+VHEAD = "lean"
+TABLE_AFTER = -1
+BIAS_AFTER = -1
+TAIL_SPLIT = {15: (256, 256,)}
+V_ADD_FROM = 999
+BIAS_Q = "scalar"
+STORE_Q = "scalar"
+TAIL_ORDER = "base"
+M_ORDER = (0, 1, 2, 3)
 
 FLOPS = 2 * 512 * 2048 * 3072
 
@@ -45,29 +61,37 @@ def tile_l1regressionmoeactionhead_pa_kernel(
         tab_pool = ctx.enter_context(tc.psum_pool(name="tab", bufs=1))
         ctx.enter_context(tc.manual_schedule())
 
-        xw = [keep.tile([P, PASSES, 512], U8, name="xw%d" % h, align_bytes=64) for h in range(2)]
-        xs = keep.tile([P, PASSES, TOKENS], U8, name="xs", align_bytes=64)
-        w0 = [keep.tile([P, 3, 2 * N_TILE], U8, name="w0%d" % h, align_bytes=64) for h in range(2)]
+        xw = [keep.tile([P, PASSES, 256 * (b - a)], U8, name="xw%d" % i, align_bytes=64) for i, (a, b) in enumerate(XW_GROUPS)]
+        xs = [keep.tile([P, PASSES, P * (b - a)], U8, name="xs%d" % i, align_bytes=64) for i, (a, b) in enumerate(XS_GROUPS)]
+        w0 = [keep.tile([P, c, 2 * N_TILE], U8, name="w0%d" % i, align_bytes=64) for i, c in enumerate(W0_SPLIT)]
         ww = [None] + [keep.tile([P, PASSES, 2 * N_TILE], U8, name="ww%d" % n, align_bytes=64) for n in range(1, N_TILES)]
         ws = [keep.tile([P, PASSES, N_TILE], U8, name="ws%d" % n, align_bytes=64) for n in range(N_TILES)]
 
         def w_codes(n, g):
             if n == 0:
-                return w0[g // 3][:, g % 3, :]
+                i = 0
+                while g >= W0_SPLIT[i]:
+                    g -= W0_SPLIT[i]
+                    i += 1
+                return w0[i][:, g, :]
             return ww[n][:, g, :]
 
+        def x_codes(m, g):
+            for i, (a, b) in enumerate(XW_GROUPS):
+                if a <= m < b:
+                    return xw[i][:, g, 256 * (m - a) : 256 * (m - a + 1)]
+            return None
+
+        def x_plane(m, g):
+            for i, (a, b) in enumerate(XS_GROUPS):
+                if a <= m < b:
+                    return xs[i][:, g, P * (m - a) : P * (m - a + 1)]
+            return None
+
         brow = keep.tile([P, N_TILE], BF16, name="brow")
-        nc.vector.memset(brow[:], 0.0)
-        zero = keep.tile([P, P], BF16, name="zero")
-        nc.vector.memset(zero[:], 0.0)
-        nc.vector.memset(xs[:].bitcast(I32), 0)
+        zero = keep.tile([P, max(P, WARM_N)], BF16, name="zero")
         turns = keep.tile([P, 2, HALF], F32, name="turns")
-        nc.gpsimd.iota(
-            turns[:, :, 0:1], pattern=[[-P, 2], [0, 1]], base=0, channel_multiplier=-1, allow_small_or_imprecise_dtypes=True
-        )
         ident = keep.tile([P, P], F32, name="ident")
-        nc.vector.memset(ident[:], 0.0)
-        make_identity(nc, ident[:], nomemset=True)
 
         def widen(w):
             for k in (1, 2, 3):
@@ -78,11 +102,48 @@ def tile_l1regressionmoeactionhead_pa_kernel(
                     out=turns[:, :, k * w : (k + 1) * w], in0=turns[:, :, 0:w], scalar1=factor, scalar2=None, op0=ALU.mult
                 )
 
-        widen(1)
-        nc.vector.memset(ws[0][:].bitcast(I32), 0)
+        def iota_turns():
+            nc.gpsimd.iota(
+                turns[:, :, 0:1], pattern=[[-P, 2], [0, 1]], base=0, channel_multiplier=-1, allow_small_or_imprecise_dtypes=True
+            )
+
+        if VHEAD == "base":
+            nc.vector.memset(brow[:], 0.0)
+            nc.vector.memset(zero[:], 0.0)
+            nc.vector.memset(xs[0][:].bitcast(I32), 0)
+            iota_turns()
+            nc.vector.memset(ident[:], 0.0)
+            make_identity(nc, ident[:], nomemset=True)
+            widen(1)
+            nc.vector.memset(ws[0][:].bitcast(I32), 0)
+        elif VHEAD == "planes_first":
+            nc.vector.memset(brow[:], 0.0)
+            nc.vector.memset(xs[0][:].bitcast(I32), 0)
+            nc.vector.memset(ws[0][:].bitcast(I32), 0)
+            nc.vector.memset(zero[:], 0.0)
+            iota_turns()
+            nc.vector.memset(ident[:], 0.0)
+            make_identity(nc, ident[:], nomemset=True)
+            widen(1)
+        elif VHEAD == "zero_planes":
+            nc.vector.memset(zero[:], 0.0)
+            nc.vector.memset(brow[:], 0.0)
+            nc.vector.memset(xs[0][:].bitcast(I32), 0)
+            nc.vector.memset(ws[0][:].bitcast(I32), 0)
+            iota_turns()
+            make_identity(nc, ident[:])
+            widen(1)
+        elif VHEAD == "lean":
+            nc.vector.memset(brow[:], 0.0)
+            nc.vector.memset(zero[:], 0.0)
+            nc.vector.memset(xs[0][:].bitcast(I32), 0)
+            iota_turns()
+            make_identity(nc, ident[:])
+            widen(1)
+            nc.vector.memset(ws[0][:].bitcast(I32), 0)
 
         def load_scales(planes, scales, c0, c1):
-            for q in range(4):
+            for q in Q_ORDER:
                 nc.sync.dma_start(
                     out=planes[32 * q : 32 * q + 4, :, :].bitcast(I32),
                     in_=scales[:, 4 * q : 4 * q + 4, c0:c1].rearrange("g r n -> r g n").bitcast(I32),
@@ -94,23 +155,34 @@ def tile_l1regressionmoeactionhead_pa_kernel(
                 in_=words[g0:g1, :, c0:c1].rearrange("g p c -> p g c").bitcast(I32),
             )
 
-        nc.scalar.dma_start(out=brow[0:2, :], in_=b_qa.rearrange("(o n) -> o n", o=2))
-        nc.scalar.dma_start(out=brow[2:4, :], in_=b_qt.rearrange("(o n) -> o n", o=2))
-        load_codes(xw[0], x_words, 0, PASSES, 0, 512)
-        load_codes(w0[0], w_words[0], 0, 3, 0, 2 * N_TILE)
-        load_scales(xs, x_scales, 0, TOKENS)
-        load_scales(ws[0], w_scales[0], 0, N_TILE)
-        load_codes(w0[1], w_words[0], 3, PASSES, 0, 2 * N_TILE)
-        load_codes(xw[1], x_words, 0, PASSES, 512, 1024)
+        bias_queue = nc.scalar if BIAS_Q == "scalar" else nc.gpsimd
+        bias_queue.dma_start(out=brow[0:2, :], in_=b_qa.rearrange("(o n) -> o n", o=2))
+        bias_queue.dma_start(out=brow[2:4, :], in_=b_qt.rearrange("(o n) -> o n", o=2))
+        def head_load(what):
+            i = int(what[-1])
+            if what.startswith("xw"):
+                a, b = XW_GROUPS[i]
+                load_codes(xw[i], x_words, 0, PASSES, 256 * a, 256 * b)
+            elif what.startswith("xs"):
+                a, b = XS_GROUPS[i]
+                load_scales(xs[i], x_scales, P * a, P * b)
+            elif what.startswith("ws"):
+                load_scales(ws[0], w_scales[0], 0, N_TILE)
+            else:
+                g0 = sum(W0_SPLIT[:i])
+                load_codes(w0[i], w_words[0], g0, g0 + W0_SPLIT[i], 0, 2 * N_TILE)
+
+        for what in HEAD_LOADS:
+            head_load(what)
 
         warm = keep.tile([P, 1], F32, name="warm")
         nc.scalar.activation(out=warm[:], in_=zero[:, 0:1], func=ACT.Sin)
         ident_bf = keep.tile([P, P], BF16, name="ident_bf")
         nc.scalar.copy(out=ident_bf[:], in_=ident[:])
 
-        junk = acc_pool.tile([P, P], F32, name="junk", tag="acc")
+        junk = acc_pool.tile([P, WARM_N], F32, name="junk", tag="acc")
         for i in range(WARM_UP):
-            nc.tensor.matmul(out=junk[:], lhsT=zero[:], rhs=zero[:], start=True, stop=True)
+            nc.tensor.matmul(out=junk[:], lhsT=zero[:, 0:P], rhs=zero[:, 0:WARM_N], start=True, stop=True)
 
         bias = keep.tile([P, 4 * N_TILE], F32, name="bias")
 
@@ -119,7 +191,6 @@ def tile_l1regressionmoeactionhead_pa_kernel(
             bp = acc_pool.tile([P, N_TILE], F32, name="bias_ps%d" % n, tag="acc")
             nc.tensor.matmul(out=bp[:], lhsT=ident_bf[:, n : n + 1].to_broadcast([P, P]), rhs=brow[:], start=True, stop=True)
             bias_ps.append(bp)
-        nc.scalar.copy(out=bias[:, 0:N_TILE], in_=bias_ps[0][:])
 
         widen(4)
         widen(16)
@@ -136,13 +207,8 @@ def tile_l1regressionmoeactionhead_pa_kernel(
             nc.vector.scalar_tensor_tensor(
                 out=frac[:, kind, :], in0=whole[:, kind, :], scalar=-2.0 * math.pi, in1=flat, op0=ALU.mult, op1=ALU.add
             )
-        for kind in range(2):
-            nc.scalar.activation(
-                out=tab[:, kind, :, :].rearrange("p m j -> p (m j)"),
-                in_=frac[:, kind, :],
-                func=ACT.Sin,
-                bias=kind * math.pi / 2.0,
-            )
+
+        def table_to_psum(kind):
             nc.tensor.matmul(
                 out=tab_ps[:, kind, :, :].rearrange("p m j -> p (m j)"),
                 lhsT=ident[:],
@@ -150,18 +216,38 @@ def tile_l1regressionmoeactionhead_pa_kernel(
                 start=True,
                 stop=True,
             )
-        for n in range(1, N_TILES):
+
+        for kind in range(2):
+            nc.scalar.activation(
+                out=tab[:, kind, :, :].rearrange("p m j -> p (m j)"),
+                in_=frac[:, kind, :],
+                func=ACT.Sin,
+                bias=kind * math.pi / 2.0,
+            )
+            if TABLE_AFTER < 0:
+                table_to_psum(kind)
+        for n in range(N_TILES):
             nc.scalar.copy(out=bias[:, n * N_TILE : (n + 1) * N_TILE], in_=bias_ps[n][:])
 
+        for t in xs[1:]:
+            nc.vector.memset(t[:].bitcast(I32), 0)
         for n in range(1, N_TILES):
             nc.vector.memset(ws[n][:].bitcast(I32), 0)
+        for what in HEAD_LOADS_2:
+            head_load(what)
         for n in range(1, N_TILES):
             c = n % 2
             load_scales(ws[n], w_scales[n // 2], c * N_TILE, (c + 1) * N_TILE)
             load_codes(ww[n], w_words[n // 2], 0, PASSES, c * 2 * N_TILE, (c + 1) * 2 * N_TILE)
 
-        units = [(n, m, 0, N_TILE) for n in range(N_TILES) for m in range(M_TILES)]
-        units = units[:-1] + [(N_TILES - 1, M_TILES - 1, 0, 256), (N_TILES - 1, M_TILES - 1, 256, 256)]
+        units = []
+        for n in range(N_TILES):
+            for m in M_ORDER:
+                widths = TAIL_SPLIT.get(len(M_ORDER) * n + M_ORDER.index(m), (N_TILE,))
+                c0 = 0
+                for w in widths:
+                    units.append((n, m, c0, w))
+                    c0 += w
         z_of = {}
         block_of = {}
 
@@ -182,13 +268,16 @@ def tile_l1regressionmoeactionhead_pa_kernel(
             for g in range(PASSES):
                 nc.tensor.matmul_mx(
                     out=acc[:],
-                    lhsT=xw[m // 2][:, g, 256 * (m % 2) : 256 * (m % 2 + 1)].bitcast(FP4X4),
-                    lhsT_scale=xs[:, g, P * m : P * (m + 1)],
+                    lhsT=x_codes(m, g).bitcast(FP4X4),
+                    lhsT_scale=x_plane(m, g),
                     rhs=w_codes(n, g)[:, 2 * c0 : 2 * (c0 + w)].bitcast(FP4X4),
                     rhs_scale=ws[n][:, g, c0 : c0 + w],
                     start=(g == 0),
                     stop=(g == PASSES - 1),
                 )
+            if k == TABLE_AFTER:
+                table_to_psum(0)
+                table_to_psum(1)
             z = work.tile([P, w], F32, name="z", tag="z", bufs=6)
             nc.vector.tensor_tensor(out=z[:], in0=acc[:], in1=bias[:, n * N_TILE + c0 : n * N_TILE + c0 + w], op=ALU.add)
             z_of[k] = z
@@ -217,6 +306,8 @@ def tile_l1regressionmoeactionhead_pa_kernel(
                 op=ALU.mult,
             )
 
+        store_queue = {"scalar": nc.scalar, "sync": nc.sync, "gpsimd": nc.gpsimd}[STORE_Q]
+
         def finish(ks, engine):
             tiles, b0 = block(ks[0])
             engine.tensor_tensor(out=tiles[2][:], in0=tiles[0][:], in1=tiles[1][:], op=ALU.add)
@@ -225,10 +316,13 @@ def tile_l1regressionmoeactionhead_pa_kernel(
                 tiles, b0 = block(k)
                 h0 = (n % 2) * 4 + c0 // HEAD
                 pt = m % 2
-                nc.scalar.dma_start(
+                store_queue.dma_start(
                     out=outs[n // 2][m // 2, h0 : h0 + w // HEAD, pt * P : (pt + 1) * P, :].rearrange("h p d -> p h d"),
                     in_=tiles[2][:, b0 : b0 + w].rearrange("p (h d) -> p h d", d=HEAD),
                 )
+
+        def adder(k):
+            return nc.vector if k >= V_ADD_FROM else nc.gpsimd
 
         last = len(units) - 1
         for k in range(len(units)):
@@ -238,7 +332,7 @@ def tile_l1regressionmoeactionhead_pa_kernel(
             times_cosine(k)
             if k > 0:
                 if k - 1 >= PAIRED_UNITS:
-                    finish([k - 1], nc.gpsimd)
+                    finish([k - 1], adder(k - 1))
                 elif (k - 1) % 2 == 1:
                     finish([k - 2, k - 1], nc.gpsimd)
         times_sine(last)

@@ -134,13 +134,13 @@ def tile_l1regressionmoeactionhead_pa_kernel(
             make_identity(nc, ident[:])
             widen(1)
         elif VHEAD == "lean":
-            nc.vector.memset(brow[:], 0.0)
-            nc.vector.memset(zero[:], 0.0)
+            nc.vector.memset(brow[:].bitcast(I32), 0)
+            nc.vector.memset(zero[:].bitcast(I32), 0)
             nc.vector.memset(xs[0][:].bitcast(I32), 0)
+            nc.vector.memset(ws[0][:].bitcast(I32), 0)
             iota_turns()
             make_identity(nc, ident[:])
             widen(1)
-            nc.vector.memset(ws[0][:].bitcast(I32), 0)
 
         def load_scales(planes, scales, c0, c1):
             for q in Q_ORDER:

@@ -29,7 +29,7 @@ Q_ORDER = (0, 2, 1, 3)
 XW_GROUPS = ((0, 1), (1, 2), (2, 4),)
 XS_GROUPS = ((0, 2), (2, 4),)
 W0_SPLIT = (2, 2, 2,)
-HEAD_LOADS = ("xw0", "w0_0", "xs0", "ws0", "w0_1", "w0_2", "xw1",)
+HEAD_LOADS = ("xh0", "w0_0", "xs0", "ws0", "xh1", "w0_1", "w0_2", "xw1",)
 HEAD_LOADS_2 = ("xs1", "xw2",)
 VHEAD = "lean"
 TABLE_AFTER = -1
@@ -62,6 +62,7 @@ def tile_l1regressionmoeactionhead_pa_kernel(
         ctx.enter_context(tc.manual_schedule())
 
         xw = [keep.tile([P, PASSES, 256 * (b - a)], U8, name="xw%d" % i, align_bytes=64) for i, (a, b) in enumerate(XW_GROUPS)]
+        xw0_half = [keep.tile([P, 3, 256], U8, name="xw0h%d" % h, align_bytes=64) for h in range(2)]
         xs = [keep.tile([P, PASSES, P * (b - a)], U8, name="xs%d" % i, align_bytes=64) for i, (a, b) in enumerate(XS_GROUPS)]
         w0 = [keep.tile([P, c, 2 * N_TILE], U8, name="w0%d" % i, align_bytes=64) for i, c in enumerate(W0_SPLIT)]
         ww = [None] + [keep.tile([P, PASSES, 2 * N_TILE], U8, name="ww%d" % n, align_bytes=64) for n in range(1, N_TILES)]
@@ -77,6 +78,8 @@ def tile_l1regressionmoeactionhead_pa_kernel(
             return ww[n][:, g, :]
 
         def x_codes(m, g):
+            if m == 0:
+                return xw0_half[g // 3][:, g % 3, :]
             for i, (a, b) in enumerate(XW_GROUPS):
                 if a <= m < b:
                     return xw[i][:, g, 256 * (m - a) : 256 * (m - a + 1)]
@@ -160,7 +163,9 @@ def tile_l1regressionmoeactionhead_pa_kernel(
         bias_queue.dma_start(out=brow[2:4, :], in_=b_qt.rearrange("(o n) -> o n", o=2))
         def head_load(what):
             i = int(what[-1])
-            if what.startswith("xw"):
+            if what.startswith("xh"):
+                load_codes(xw0_half[i], x_words, 3 * i, 3 * i + 3, 0, 256)
+            elif what.startswith("xw"):
                 a, b = XW_GROUPS[i]
                 load_codes(xw[i], x_words, 0, PASSES, 256 * a, 256 * b)
             elif what.startswith("xs"):
@@ -316,7 +321,8 @@ def tile_l1regressionmoeactionhead_pa_kernel(
                 tiles, b0 = block(k)
                 h0 = (n % 2) * 4 + c0 // HEAD
                 pt = m % 2
-                store_queue.dma_start(
+                queue = nc.sync if k == len(units) - 1 else store_queue
+                queue.dma_start(
                     out=outs[n // 2][m // 2, h0 : h0 + w // HEAD, pt * P : (pt + 1) * P, :].rearrange("h p d -> p h d"),
                     in_=tiles[2][:, b0 : b0 + w].rearrange("p (h d) -> p h d", d=HEAD),
                 )

@@ -61,12 +61,12 @@ def tile_l1regressionmoeactionhead_pa_kernel(
         tab_pool = ctx.enter_context(tc.psum_pool(name="tab", bufs=1))
         ctx.enter_context(tc.manual_schedule())
 
-        xw = [keep.tile([P, PASSES, 256 * (b - a)], U8, name="xw%d" % i, align_bytes=64) for i, (a, b) in enumerate(XW_GROUPS)]
-        xw0_half = [keep.tile([P, 3, 256], U8, name="xw0h%d" % h, align_bytes=64) for h in range(2)]
-        xs = [keep.tile([P, PASSES, P * (b - a)], U8, name="xs%d" % i, align_bytes=64) for i, (a, b) in enumerate(XS_GROUPS)]
-        w0 = [keep.tile([P, c, 2 * N_TILE], U8, name="w0%d" % i, align_bytes=64) for i, c in enumerate(W0_SPLIT)]
-        ww = [None] + [keep.tile([P, PASSES, 2 * N_TILE], U8, name="ww%d" % n, align_bytes=64) for n in range(1, N_TILES)]
-        ws = [keep.tile([P, PASSES, N_TILE], U8, name="ws%d" % n, align_bytes=64) for n in range(N_TILES)]
+        xw = [keep.tile([P, PASSES, 256 * (b - a)], U8, name="xw%d" % i, align_bytes=256) for i, (a, b) in enumerate(XW_GROUPS)]
+        xw0_half = [keep.tile([P, 3, 256], U8, name="xw0h%d" % h, align_bytes=256) for h in range(2)]
+        xs = [keep.tile([P, PASSES, P * (b - a)], U8, name="xs%d" % i, align_bytes=256) for i, (a, b) in enumerate(XS_GROUPS)]
+        w0 = [keep.tile([P, c, 2 * N_TILE], U8, name="w0%d" % i, align_bytes=256) for i, c in enumerate(W0_SPLIT)]
+        ww = [None] + [keep.tile([P, PASSES, 2 * N_TILE], U8, name="ww%d" % n, align_bytes=256) for n in range(1, N_TILES)]
+        ws = [keep.tile([P, PASSES, N_TILE], U8, name="ws%d" % n, align_bytes=256) for n in range(N_TILES)]
 
         def w_codes(n, g):
             if n == 0:
@@ -85,7 +85,11 @@ def tile_l1regressionmoeactionhead_pa_kernel(
                     return xw[i][:, g, 256 * (m - a) : 256 * (m - a + 1)]
             return None
 
+        x_odd = {m: keep.tile([P, PASSES, 256], U8, name="x_odd%d" % m, align_bytes=256) for m in (1, 3)}
+
         def x_plane(m, g):
+            if m in x_odd:
+                return x_odd[m][:, g, 0:P]
             for i, (a, b) in enumerate(XS_GROUPS):
                 if a <= m < b:
                     return xs[i][:, g, P * (m - a) : P * (m - a + 1)]
@@ -244,6 +248,11 @@ def tile_l1regressionmoeactionhead_pa_kernel(
             c = n % 2
             load_scales(ws[n], w_scales[n // 2], c * N_TILE, (c + 1) * N_TILE)
             load_codes(ww[n], w_words[n // 2], 0, PASSES, c * 2 * N_TILE, (c + 1) * 2 * N_TILE)
+
+        for m in (1, 3):
+            nc.gpsimd.tensor_copy(
+                out=x_odd[m][:, :, 0:P].bitcast(I32), in_=xs[m // 2][:, :, P : 2 * P].bitcast(I32)
+            )
 
         units = []
         for n in range(N_TILES):

@@ -85,11 +85,7 @@ def tile_l1regressionmoeactionhead_pa_kernel(
                     return xw[i][:, g, 256 * (m - a) : 256 * (m - a + 1)]
             return None
 
-        x_odd = {m: keep.tile([P, PASSES, 256], U8, name="x_odd%d" % m, align_bytes=256) for m in (1, 3)}
-
         def x_plane(m, g):
-            if m in x_odd:
-                return x_odd[m][:, g, 0:P]
             for i, (a, b) in enumerate(XS_GROUPS):
                 if a <= m < b:
                     return xs[i][:, g, P * (m - a) : P * (m - a + 1)]
@@ -248,11 +244,6 @@ def tile_l1regressionmoeactionhead_pa_kernel(
             c = n % 2
             load_scales(ws[n], w_scales[n // 2], c * N_TILE, (c + 1) * N_TILE)
             load_codes(ww[n], w_words[n // 2], 0, PASSES, c * 2 * N_TILE, (c + 1) * 2 * N_TILE)
-
-        for m in (1, 3):
-            nc.gpsimd.tensor_copy(
-                out=x_odd[m][:, :, 0:P].bitcast(I32), in_=xs[m // 2][:, :, P : 2 * P].bitcast(I32)
-            )
 
         units = []
         for n in range(N_TILES):

@@ -14,36 +14,24 @@ ACT = mybir.ActivationFunctionType
 
 P = 128
 PASSES = 6
-TOKENS = 512
-M_TILES = 4
-N_TILE = 512
-N_TILES = 4
+TOKEN_TILES = 4
+COLUMNS = 512
+COLUMN_TILES = 4
 HEAD = 128
 HALF = 64
+RATIO = 10000.0 ** (-1.0 / 64.0)
+
+ALIGN = 256
+
+QUADRANT_ORDER = (0, 2, 1, 3)
+
 WARM_UP = 12
-WARM_N = 128
-PAIRED_UNITS = 8
+
 GPSIMD_COSINE_UNITS = (3, 8)
-SBUF_TABLE_UNITS = 0
-Q_ORDER = (0, 2, 1, 3)
-XW_GROUPS = ((0, 1), (1, 2), (2, 4),)
-XS_GROUPS = ((0, 2), (2, 4),)
-W0_SPLIT = (2, 2, 2,)
-HEAD_LOADS = ("xh0", "w0_0", "xs0", "ws0", "xh1", "w0_1", "w0_2", "xw1",)
-HEAD_LOADS_2 = ("xs1", "xw2",)
-VHEAD = "lean"
-TABLE_AFTER = -1
-BIAS_AFTER = -1
-TAIL_SPLIT = {15: (256, 256,)}
-V_ADD_FROM = 999
-BIAS_Q = "scalar"
-STORE_Q = "scalar"
-TAIL_ORDER = "base"
-M_ORDER = (0, 1, 2, 3)
+
+PAIRED_UNITS = 8
 
 FLOPS = 2 * 512 * 2048 * 3072
-
-RATIO = 10000.0 ** (-1.0 / 64.0)
 
 
 def tile_l1regressionmoeactionhead_pa_kernel(
@@ -61,40 +49,35 @@ def tile_l1regressionmoeactionhead_pa_kernel(
         tab_pool = ctx.enter_context(tc.psum_pool(name="tab", bufs=1))
         ctx.enter_context(tc.manual_schedule())
 
-        xw = [keep.tile([P, PASSES, 256 * (b - a)], U8, name="xw%d" % i, align_bytes=256) for i, (a, b) in enumerate(XW_GROUPS)]
-        xw0_half = [keep.tile([P, 3, 256], U8, name="xw0h%d" % h, align_bytes=256) for h in range(2)]
-        xs = [keep.tile([P, PASSES, P * (b - a)], U8, name="xs%d" % i, align_bytes=256) for i, (a, b) in enumerate(XS_GROUPS)]
-        w0 = [keep.tile([P, c, 2 * N_TILE], U8, name="w0%d" % i, align_bytes=256) for i, c in enumerate(W0_SPLIT)]
-        ww = [None] + [keep.tile([P, PASSES, 2 * N_TILE], U8, name="ww%d" % n, align_bytes=256) for n in range(1, N_TILES)]
-        ws = [keep.tile([P, PASSES, N_TILE], U8, name="ws%d" % n, align_bytes=256) for n in range(N_TILES)]
+        x0_codes = [keep.tile([P, 3, 256], U8, name="x0_codes%d" % h, align_bytes=ALIGN) for h in range(2)]
+        x1_codes = keep.tile([P, PASSES, 256], U8, name="x1_codes", align_bytes=ALIGN)
+        x23_codes = keep.tile([P, PASSES, 512], U8, name="x23_codes", align_bytes=ALIGN)
+        x_planes = [keep.tile([P, PASSES, 2 * P], U8, name="x_planes%d" % i, align_bytes=ALIGN) for i in range(2)]
+        w0_codes = [keep.tile([P, 2, 2 * COLUMNS], U8, name="w0_codes%d" % i, align_bytes=ALIGN) for i in range(3)]
+        w_codes = [None] + [
+            keep.tile([P, PASSES, 2 * COLUMNS], U8, name="w_codes%d" % n, align_bytes=ALIGN) for n in range(1, COLUMN_TILES)
+        ]
+        w_planes = [keep.tile([P, PASSES, COLUMNS], U8, name="w_planes%d" % n, align_bytes=ALIGN) for n in range(COLUMN_TILES)]
 
-        def w_codes(n, g):
-            if n == 0:
-                i = 0
-                while g >= W0_SPLIT[i]:
-                    g -= W0_SPLIT[i]
-                    i += 1
-                return w0[i][:, g, :]
-            return ww[n][:, g, :]
-
-        def x_codes(m, g):
+        def stationary_codes(m, g):
             if m == 0:
-                return xw0_half[g // 3][:, g % 3, :]
-            for i, (a, b) in enumerate(XW_GROUPS):
-                if a <= m < b:
-                    return xw[i][:, g, 256 * (m - a) : 256 * (m - a + 1)]
-            return None
+                return x0_codes[g // 3][:, g % 3, :]
+            if m == 1:
+                return x1_codes[:, g, :]
+            return x23_codes[:, g, 256 * (m - 2) : 256 * (m - 1)]
 
-        def x_plane(m, g):
-            for i, (a, b) in enumerate(XS_GROUPS):
-                if a <= m < b:
-                    return xs[i][:, g, P * (m - a) : P * (m - a + 1)]
-            return None
+        def stationary_scales(m, g):
+            return x_planes[m // 2][:, g, P * (m % 2) : P * (m % 2 + 1)]
 
-        brow = keep.tile([P, N_TILE], BF16, name="brow")
-        zero = keep.tile([P, max(P, WARM_N)], BF16, name="zero")
-        turns = keep.tile([P, 2, HALF], F32, name="turns")
-        ident = keep.tile([P, P], F32, name="ident")
+        def moving_codes(n, g):
+            if n == 0:
+                return w0_codes[g // 2][:, g % 2, :]
+            return w_codes[n][:, g, :]
+
+        bias_rows = keep.tile([P, COLUMNS], BF16, name="bias_rows", align_bytes=ALIGN)
+        zeros = keep.tile([P, P], BF16, name="zeros", align_bytes=ALIGN)
+        angles = keep.tile([P, 2, HALF], F32, name="angles", align_bytes=ALIGN)
+        ident = keep.tile([P, P], F32, name="ident", align_bytes=ALIGN)
 
         def widen(w):
             for k in (1, 2, 3):
@@ -102,170 +85,120 @@ def tile_l1regressionmoeactionhead_pa_kernel(
                 if (k * w) % 2 == 1:
                     factor = -factor
                 nc.vector.tensor_scalar(
-                    out=turns[:, :, k * w : (k + 1) * w], in0=turns[:, :, 0:w], scalar1=factor, scalar2=None, op0=ALU.mult
+                    out=angles[:, :, k * w : (k + 1) * w], in0=angles[:, :, 0:w], scalar1=factor, scalar2=None, op0=ALU.mult
                 )
 
-        def iota_turns():
-            nc.gpsimd.iota(
-                turns[:, :, 0:1], pattern=[[-P, 2], [0, 1]], base=0, channel_multiplier=-1, allow_small_or_imprecise_dtypes=True
-            )
-
-        if VHEAD == "base":
-            nc.vector.memset(brow[:], 0.0)
-            nc.vector.memset(zero[:], 0.0)
-            nc.vector.memset(xs[0][:].bitcast(I32), 0)
-            iota_turns()
-            nc.vector.memset(ident[:], 0.0)
-            make_identity(nc, ident[:], nomemset=True)
-            widen(1)
-            nc.vector.memset(ws[0][:].bitcast(I32), 0)
-        elif VHEAD == "planes_first":
-            nc.vector.memset(brow[:], 0.0)
-            nc.vector.memset(xs[0][:].bitcast(I32), 0)
-            nc.vector.memset(ws[0][:].bitcast(I32), 0)
-            nc.vector.memset(zero[:], 0.0)
-            iota_turns()
-            nc.vector.memset(ident[:], 0.0)
-            make_identity(nc, ident[:], nomemset=True)
-            widen(1)
-        elif VHEAD == "zero_planes":
-            nc.vector.memset(zero[:], 0.0)
-            nc.vector.memset(brow[:], 0.0)
-            nc.vector.memset(xs[0][:].bitcast(I32), 0)
-            nc.vector.memset(ws[0][:].bitcast(I32), 0)
-            iota_turns()
-            make_identity(nc, ident[:])
-            widen(1)
-        elif VHEAD == "lean":
-            nc.vector.memset(brow[:].bitcast(I32), 0)
-            nc.vector.memset(zero[:].bitcast(I32), 0)
-            nc.vector.memset(xs[0][:].bitcast(I32), 0)
-            nc.vector.memset(ws[0][:].bitcast(I32), 0)
-            iota_turns()
-            make_identity(nc, ident[:])
-            widen(1)
+        nc.vector.memset(bias_rows[:].bitcast(I32), 0)
+        nc.vector.memset(zeros[:].bitcast(I32), 0)
+        nc.vector.memset(x_planes[0][:].bitcast(I32), 0)
+        nc.vector.memset(w_planes[0][:].bitcast(I32), 0)
+        nc.gpsimd.iota(
+            angles[:, :, 0:1], pattern=[[-P, 2], [0, 1]], base=0, channel_multiplier=-1, allow_small_or_imprecise_dtypes=True
+        )
+        make_identity(nc, ident[:])
+        widen(1)
 
         def load_scales(planes, scales, c0, c1):
-            for q in Q_ORDER:
+            for q in QUADRANT_ORDER:
                 nc.sync.dma_start(
                     out=planes[32 * q : 32 * q + 4, :, :].bitcast(I32),
                     in_=scales[:, 4 * q : 4 * q + 4, c0:c1].rearrange("g r n -> r g n").bitcast(I32),
                 )
 
-        def load_codes(tile_ap, words, g0, g1, c0, c1):
+        def load_codes(codes, words, g0, g1, c0, c1):
             nc.sync.dma_start(
-                out=tile_ap[:].bitcast(I32),
+                out=codes[:].bitcast(I32),
                 in_=words[g0:g1, :, c0:c1].rearrange("g p c -> p g c").bitcast(I32),
             )
 
-        bias_queue = nc.scalar if BIAS_Q == "scalar" else nc.gpsimd
-        bias_queue.dma_start(out=brow[0:2, :], in_=b_qa.rearrange("(o n) -> o n", o=2))
-        bias_queue.dma_start(out=brow[2:4, :], in_=b_qt.rearrange("(o n) -> o n", o=2))
-        def head_load(what):
-            i = int(what[-1])
-            if what.startswith("xh"):
-                load_codes(xw0_half[i], x_words, 3 * i, 3 * i + 3, 0, 256)
-            elif what.startswith("xw"):
-                a, b = XW_GROUPS[i]
-                load_codes(xw[i], x_words, 0, PASSES, 256 * a, 256 * b)
-            elif what.startswith("xs"):
-                a, b = XS_GROUPS[i]
-                load_scales(xs[i], x_scales, P * a, P * b)
-            elif what.startswith("ws"):
-                load_scales(ws[0], w_scales[0], 0, N_TILE)
-            else:
-                g0 = sum(W0_SPLIT[:i])
-                load_codes(w0[i], w_words[0], g0, g0 + W0_SPLIT[i], 0, 2 * N_TILE)
+        nc.scalar.dma_start(out=bias_rows[0:2, :], in_=b_qa.rearrange("(o n) -> o n", o=2))
+        nc.scalar.dma_start(out=bias_rows[2:4, :], in_=b_qt.rearrange("(o n) -> o n", o=2))
+        load_codes(x0_codes[0], x_words, 0, 3, 0, 256)
+        load_codes(w0_codes[0], w_words[0], 0, 2, 0, 2 * COLUMNS)
+        load_scales(x_planes[0], x_scales, 0, 2 * P)
+        load_scales(w_planes[0], w_scales[0], 0, COLUMNS)
+        load_codes(x0_codes[1], x_words, 3, PASSES, 0, 256)
+        load_codes(w0_codes[1], w_words[0], 2, 4, 0, 2 * COLUMNS)
+        load_codes(w0_codes[2], w_words[0], 4, PASSES, 0, 2 * COLUMNS)
+        load_codes(x1_codes, x_words, 0, PASSES, 256, 512)
 
-        for what in HEAD_LOADS:
-            head_load(what)
-
-        warm = keep.tile([P, 1], F32, name="warm")
-        nc.scalar.activation(out=warm[:], in_=zero[:, 0:1], func=ACT.Sin)
-        ident_bf = keep.tile([P, P], BF16, name="ident_bf")
+        table_load = keep.tile([P, 1], F32, name="table_load", align_bytes=ALIGN)
+        nc.scalar.activation(out=table_load[:], in_=zeros[:, 0:1], func=ACT.Sin)
+        ident_bf = keep.tile([P, P], BF16, name="ident_bf", align_bytes=ALIGN)
         nc.scalar.copy(out=ident_bf[:], in_=ident[:])
 
-        junk = acc_pool.tile([P, WARM_N], F32, name="junk", tag="acc")
+        warm_up_out = acc_pool.tile([P, P], F32, name="warm_up_out", tag="acc")
         for i in range(WARM_UP):
-            nc.tensor.matmul(out=junk[:], lhsT=zero[:, 0:P], rhs=zero[:, 0:WARM_N], start=True, stop=True)
+            nc.tensor.matmul(out=warm_up_out[:], lhsT=zeros[:], rhs=zeros[:], start=True, stop=True)
 
-        bias = keep.tile([P, 4 * N_TILE], F32, name="bias")
-
-        bias_ps = []
-        for n in range(N_TILES):
-            bp = acc_pool.tile([P, N_TILE], F32, name="bias_ps%d" % n, tag="acc")
-            nc.tensor.matmul(out=bp[:], lhsT=ident_bf[:, n : n + 1].to_broadcast([P, P]), rhs=brow[:], start=True, stop=True)
-            bias_ps.append(bp)
+        bias = keep.tile([P, COLUMN_TILES * COLUMNS], F32, name="bias", align_bytes=ALIGN)
+        bias_banks = []
+        for n in range(COLUMN_TILES):
+            bank = acc_pool.tile([P, COLUMNS], F32, name="bias_bank%d" % n, tag="acc")
+            nc.tensor.matmul(
+                out=bank[:], lhsT=ident_bf[:, n : n + 1].to_broadcast([P, P]), rhs=bias_rows[:], start=True, stop=True
+            )
+            bias_banks.append(bank)
 
         widen(4)
         widen(16)
-        flat = turns[:].rearrange("p m j -> p (m j)")
-        whole = keep.tile([P, 2, 2 * HALF], I32, name="whole")
-        nc.vector.tensor_scalar(out=whole[:, 0, :], in0=flat, scalar1=1.0 / (2.0 * math.pi), scalar2=None, op0=ALU.mult)
+        flat = angles[:].rearrange("p m j -> p (m j)")
+        turns = keep.tile([P, 2, 2 * HALF], I32, name="turns", align_bytes=ALIGN)
+        nc.vector.tensor_scalar(out=turns[:, 0, :], in0=flat, scalar1=1.0 / (2.0 * math.pi), scalar2=None, op0=ALU.mult)
         nc.vector.tensor_scalar(
-            out=whole[:, 1, :], in0=flat, scalar1=1.0 / (2.0 * math.pi), scalar2=0.25, op0=ALU.mult, op1=ALU.add
+            out=turns[:, 1, :], in0=flat, scalar1=1.0 / (2.0 * math.pi), scalar2=0.25, op0=ALU.mult, op1=ALU.add
         )
-        frac = keep.tile([P, 2, 2 * HALF], F32, name="frac")
-        tab = keep.tile([P, 2, 2, HALF], F32, name="tab")
-        tab_ps = tab_pool.tile([P, 2, 2, HALF], F32, name="tab_ps")
+        reduced = keep.tile([P, 2, 2 * HALF], F32, name="reduced", align_bytes=ALIGN)
+        tables = keep.tile([P, 2, 2, HALF], F32, name="tables", align_bytes=ALIGN)
+        tables_psum = tab_pool.tile([P, 2, 2, HALF], F32, name="tables_psum")
         for kind in range(2):
             nc.vector.scalar_tensor_tensor(
-                out=frac[:, kind, :], in0=whole[:, kind, :], scalar=-2.0 * math.pi, in1=flat, op0=ALU.mult, op1=ALU.add
+                out=reduced[:, kind, :], in0=turns[:, kind, :], scalar=-2.0 * math.pi, in1=flat, op0=ALU.mult, op1=ALU.add
             )
-
-        def table_to_psum(kind):
-            nc.tensor.matmul(
-                out=tab_ps[:, kind, :, :].rearrange("p m j -> p (m j)"),
-                lhsT=ident[:],
-                rhs=tab[:, kind, :, :].rearrange("p m j -> p (m j)"),
-                start=True,
-                stop=True,
-            )
-
         for kind in range(2):
             nc.scalar.activation(
-                out=tab[:, kind, :, :].rearrange("p m j -> p (m j)"),
-                in_=frac[:, kind, :],
+                out=tables[:, kind, :, :].rearrange("p m j -> p (m j)"),
+                in_=reduced[:, kind, :],
                 func=ACT.Sin,
                 bias=kind * math.pi / 2.0,
             )
-            if TABLE_AFTER < 0:
-                table_to_psum(kind)
-        for n in range(N_TILES):
-            nc.scalar.copy(out=bias[:, n * N_TILE : (n + 1) * N_TILE], in_=bias_ps[n][:])
+            nc.tensor.matmul(
+                out=tables_psum[:, kind, :, :].rearrange("p m j -> p (m j)"),
+                lhsT=ident[:],
+                rhs=tables[:, kind, :, :].rearrange("p m j -> p (m j)"),
+                start=True,
+                stop=True,
+            )
+        for n in range(COLUMN_TILES):
+            nc.scalar.copy(out=bias[:, n * COLUMNS : (n + 1) * COLUMNS], in_=bias_banks[n][:])
 
-        for t in xs[1:]:
-            nc.vector.memset(t[:].bitcast(I32), 0)
-        for n in range(1, N_TILES):
-            nc.vector.memset(ws[n][:].bitcast(I32), 0)
-        for what in HEAD_LOADS_2:
-            head_load(what)
-        for n in range(1, N_TILES):
+        nc.vector.memset(x_planes[1][:].bitcast(I32), 0)
+        for n in range(1, COLUMN_TILES):
+            nc.vector.memset(w_planes[n][:].bitcast(I32), 0)
+        load_scales(x_planes[1], x_scales, 2 * P, 4 * P)
+        load_codes(x23_codes, x_words, 0, PASSES, 512, 1024)
+        for n in range(1, COLUMN_TILES):
             c = n % 2
-            load_scales(ws[n], w_scales[n // 2], c * N_TILE, (c + 1) * N_TILE)
-            load_codes(ww[n], w_words[n // 2], 0, PASSES, c * 2 * N_TILE, (c + 1) * 2 * N_TILE)
+            load_scales(w_planes[n], w_scales[n // 2], c * COLUMNS, (c + 1) * COLUMNS)
+            load_codes(w_codes[n], w_words[n // 2], 0, PASSES, c * 2 * COLUMNS, (c + 1) * 2 * COLUMNS)
 
-        units = []
-        for n in range(N_TILES):
-            for m in M_ORDER:
-                widths = TAIL_SPLIT.get(len(M_ORDER) * n + M_ORDER.index(m), (N_TILE,))
-                c0 = 0
-                for w in widths:
-                    units.append((n, m, c0, w))
-                    c0 += w
+        units = [(n, m, 0, COLUMNS) for n in range(COLUMN_TILES) for m in range(TOKEN_TILES)]
+        units = units[:-1] + [(COLUMN_TILES - 1, TOKEN_TILES - 1, c0, COLUMNS // 2) for c0 in (0, COLUMNS // 2)]
+        last = len(units) - 1
         z_of = {}
         block_of = {}
 
         def block(k):
-            key = k // 2 if k < PAIRED_UNITS else PAIRED_UNITS + k
+            paired = k < PAIRED_UNITS
+            key = k // 2 if paired else k
             if key not in block_of:
-                width = 2 * N_TILE if k < PAIRED_UNITS else units[k][3]
-                kind = "2" if k < PAIRED_UNITS else "1"
+                width = 2 * COLUMNS if paired else units[k][3]
+                suffix = "2" if paired else "1"
                 block_of[key] = [
-                    work.tile([P, width], F32, name=nm + kind, tag=nm + kind, bufs=5) for nm in ("zc", "zs", "res")
+                    work.tile([P, width], F32, name=nm + suffix, tag=nm + suffix, bufs=5, align_bytes=ALIGN)
+                    for nm in ("zc", "zs", "res")
                 ]
-            c0 = (k % 2) * N_TILE if k < PAIRED_UNITS else 0
-            return block_of[key], c0
+            return block_of[key], (k % 2) * COLUMNS if paired else 0
 
         def project(k):
             n, m, c0, w = units[k]
@@ -273,18 +206,15 @@ def tile_l1regressionmoeactionhead_pa_kernel(
             for g in range(PASSES):
                 nc.tensor.matmul_mx(
                     out=acc[:],
-                    lhsT=x_codes(m, g).bitcast(FP4X4),
-                    lhsT_scale=x_plane(m, g),
-                    rhs=w_codes(n, g)[:, 2 * c0 : 2 * (c0 + w)].bitcast(FP4X4),
-                    rhs_scale=ws[n][:, g, c0 : c0 + w],
+                    lhsT=stationary_codes(m, g).bitcast(FP4X4),
+                    lhsT_scale=stationary_scales(m, g),
+                    rhs=moving_codes(n, g)[:, 2 * c0 : 2 * (c0 + w)].bitcast(FP4X4),
+                    rhs_scale=w_planes[n][:, g, c0 : c0 + w],
                     start=(g == 0),
                     stop=(g == PASSES - 1),
                 )
-            if k == TABLE_AFTER:
-                table_to_psum(0)
-                table_to_psum(1)
-            z = work.tile([P, w], F32, name="z", tag="z", bufs=6)
-            nc.vector.tensor_tensor(out=z[:], in0=acc[:], in1=bias[:, n * N_TILE + c0 : n * N_TILE + c0 + w], op=ALU.add)
+            z = work.tile([P, w], F32, name="z", tag="z", bufs=6, align_bytes=ALIGN)
+            nc.vector.tensor_tensor(out=z[:], in0=acc[:], in1=bias[:, n * COLUMNS + c0 : n * COLUMNS + c0 + w], op=ALU.add)
             z_of[k] = z
 
         def times_cosine(k):
@@ -292,7 +222,7 @@ def tile_l1regressionmoeactionhead_pa_kernel(
             tiles, b0 = block(k)
             on_gpsimd = k in GPSIMD_COSINE_UNITS
             engine = nc.gpsimd if on_gpsimd else nc.vector
-            table = tab if (on_gpsimd or k < SBUF_TABLE_UNITS) else tab_ps
+            table = tables if on_gpsimd else tables_psum
             engine.tensor_tensor(
                 out=tiles[0][:, b0 : b0 + w].rearrange("p (c j) -> p c j", j=HALF),
                 in0=z_of[k][:].rearrange("p (c j) -> p c j", j=HALF),
@@ -303,15 +233,15 @@ def tile_l1regressionmoeactionhead_pa_kernel(
         def times_sine(k):
             n, m, c0, w = units[k]
             tiles, b0 = block(k)
-            table = tab if k < SBUF_TABLE_UNITS else tab_ps
             nc.vector.tensor_tensor(
                 out=tiles[1][:, b0 : b0 + w].rearrange("p (c i t) -> p c i t", i=HALF // 2, t=2),
                 in0=z_of[k][:].rearrange("p (c i t) -> p c i t", i=HALF // 2, t=2)[:, :, :, ::-1],
-                in1=table[:, 0, m % 2, :].rearrange("p (i t) -> p i t", t=2).unsqueeze(1).to_broadcast([P, w // HALF, HALF // 2, 2]),
+                in1=tables_psum[:, 0, m % 2, :]
+                .rearrange("p (i t) -> p i t", t=2)
+                .unsqueeze(1)
+                .to_broadcast([P, w // HALF, HALF // 2, 2]),
                 op=ALU.mult,
             )
-
-        store_queue = {"scalar": nc.scalar, "sync": nc.sync, "gpsimd": nc.gpsimd}[STORE_Q]
 
         def finish(ks, engine):
             tiles, b0 = block(ks[0])
@@ -320,17 +250,13 @@ def tile_l1regressionmoeactionhead_pa_kernel(
                 n, m, c0, w = units[k]
                 tiles, b0 = block(k)
                 h0 = (n % 2) * 4 + c0 // HEAD
-                pt = m % 2
-                queue = nc.sync if k == len(units) - 1 else store_queue
+                pos0 = (m % 2) * P
+                queue = nc.sync if k == last else nc.scalar
                 queue.dma_start(
-                    out=outs[n // 2][m // 2, h0 : h0 + w // HEAD, pt * P : (pt + 1) * P, :].rearrange("h p d -> p h d"),
+                    out=outs[n // 2][m // 2, h0 : h0 + w // HEAD, pos0 : pos0 + P, :].rearrange("h p d -> p h d"),
                     in_=tiles[2][:, b0 : b0 + w].rearrange("p (h d) -> p h d", d=HEAD),
                 )
 
-        def adder(k):
-            return nc.vector if k >= V_ADD_FROM else nc.gpsimd
-
-        last = len(units) - 1
         for k in range(len(units)):
             project(k)
             if k > 0:
@@ -338,7 +264,7 @@ def tile_l1regressionmoeactionhead_pa_kernel(
             times_cosine(k)
             if k > 0:
                 if k - 1 >= PAIRED_UNITS:
-                    finish([k - 1], adder(k - 1))
+                    finish([k - 1], nc.gpsimd)
                 elif (k - 1) % 2 == 1:
                     finish([k - 2, k - 1], nc.gpsimd)
         times_sine(last)

import math
from contextlib import ExitStack

import concourse.mybir as mybir
from concourse.masks import make_identity

F32 = mybir.dt.float32
BF16 = mybir.dt.bfloat16
I32 = mybir.dt.int32
U8 = mybir.dt.uint8
FP4X4 = mybir.dt.float4_e2m1fn_x4
ALU = mybir.AluOpType
ACT = mybir.ActivationFunctionType

P = 128
PASSES = 6
TOKEN_TILES = 4
COLUMNS = 512
COLUMN_TILES = 4
HEAD = 128
HALF = 64
RATIO = 10000.0 ** (-1.0 / 64.0)

ALIGN = 256

QUADRANT_ORDER = (0, 2, 1, 3)

WARM_UP = 12

GPSIMD_COSINE_UNITS = (3, 8)

PAIRED_UNITS = 8

FLOPS = 2 * 512 * 2048 * 3072


def tile_l1regressionmoeactionhead_pa_kernel(
    tc, x_words, x_scales, W_qa_words, W_qa_scales, b_qa, W_qt_words, W_qt_scales, b_qt, out_0, out_1
):
    nc = tc.nc
    w_words = (W_qa_words, W_qt_words)
    w_scales = (W_qa_scales, W_qt_scales)
    outs = (out_0, out_1)

    with ExitStack() as ctx:
        keep = ctx.enter_context(tc.tile_pool(name="keep", bufs=1))
        work = ctx.enter_context(tc.tile_pool(name="work", bufs=3))
        acc_pool = ctx.enter_context(tc.psum_pool(name="acc", bufs=7))
        tab_pool = ctx.enter_context(tc.psum_pool(name="tab", bufs=1))
        ctx.enter_context(tc.manual_schedule())

        x0_codes = [keep.tile([P, 3, 256], U8, name="x0_codes%d" % h, align_bytes=ALIGN) for h in range(2)]
        x1_codes = keep.tile([P, PASSES, 256], U8, name="x1_codes", align_bytes=ALIGN)
        x23_codes = keep.tile([P, PASSES, 512], U8, name="x23_codes", align_bytes=ALIGN)
        x_planes = [keep.tile([P, PASSES, 2 * P], U8, name="x_planes%d" % i, align_bytes=ALIGN) for i in range(2)]
        w0_codes = [keep.tile([P, 2, 2 * COLUMNS], U8, name="w0_codes%d" % i, align_bytes=ALIGN) for i in range(3)]
        w_codes = [None] + [
            keep.tile([P, PASSES, 2 * COLUMNS], U8, name="w_codes%d" % n, align_bytes=ALIGN) for n in range(1, COLUMN_TILES)
        ]
        w_planes = [keep.tile([P, PASSES, COLUMNS], U8, name="w_planes%d" % n, align_bytes=ALIGN) for n in range(COLUMN_TILES)]

        def stationary_codes(m, g):
            if m == 0:
                return x0_codes[g // 3][:, g % 3, :]
            if m == 1:
                return x1_codes[:, g, :]
            return x23_codes[:, g, 256 * (m - 2) : 256 * (m - 1)]

        def stationary_scales(m, g):
            return x_planes[m // 2][:, g, P * (m % 2) : P * (m % 2 + 1)]

        def moving_codes(n, g):
            if n == 0:
                return w0_codes[g // 2][:, g % 2, :]
            return w_codes[n][:, g, :]

        bias_rows = keep.tile([P, COLUMNS], BF16, name="bias_rows", align_bytes=ALIGN)
        zeros = keep.tile([P, P], BF16, name="zeros", align_bytes=ALIGN)
        angles = keep.tile([P, 2, HALF], F32, name="angles", align_bytes=ALIGN)
        ident = keep.tile([P, P], F32, name="ident", align_bytes=ALIGN)

        def widen(w):
            for k in (1, 2, 3):
                factor = RATIO ** (k * w)
                if (k * w) % 2 == 1:
                    factor = -factor
                nc.vector.tensor_scalar(
                    out=angles[:, :, k * w : (k + 1) * w], in0=angles[:, :, 0:w], scalar1=factor, scalar2=None, op0=ALU.mult
                )

        nc.vector.memset(bias_rows[:].bitcast(I32), 0)
        nc.vector.memset(zeros[:].bitcast(I32), 0)
        nc.vector.memset(x_planes[0][:].bitcast(I32), 0)
        nc.vector.memset(w_planes[0][:].bitcast(I32), 0)
        nc.gpsimd.iota(
            angles[:, :, 0:1], pattern=[[-P, 2], [0, 1]], base=0, channel_multiplier=-1, allow_small_or_imprecise_dtypes=True
        )
        make_identity(nc, ident[:])
        widen(1)

        def load_scales(planes, scales, c0, c1):
            for q in QUADRANT_ORDER:
                nc.sync.dma_start(
                    out=planes[32 * q : 32 * q + 4, :, :].bitcast(I32),
                    in_=scales[:, 4 * q : 4 * q + 4, c0:c1].rearrange("g r n -> r g n").bitcast(I32),
                )

        def load_codes(codes, words, g0, g1, c0, c1):
            nc.sync.dma_start(
                out=codes[:].bitcast(I32),
                in_=words[g0:g1, :, c0:c1].rearrange("g p c -> p g c").bitcast(I32),
            )

        nc.scalar.dma_start(out=bias_rows[0:2, :], in_=b_qa.rearrange("(o n) -> o n", o=2))
        nc.scalar.dma_start(out=bias_rows[2:4, :], in_=b_qt.rearrange("(o n) -> o n", o=2))
        load_codes(x0_codes[0], x_words, 0, 3, 0, 256)
        load_codes(w0_codes[0], w_words[0], 0, 2, 0, 2 * COLUMNS)
        load_scales(x_planes[0], x_scales, 0, 2 * P)
        load_scales(w_planes[0], w_scales[0], 0, COLUMNS)
        load_codes(x0_codes[1], x_words, 3, PASSES, 0, 256)
        load_codes(w0_codes[1], w_words[0], 2, 4, 0, 2 * COLUMNS)
        load_codes(w0_codes[2], w_words[0], 4, PASSES, 0, 2 * COLUMNS)
        load_codes(x1_codes, x_words, 0, PASSES, 256, 512)

        table_load = keep.tile([P, 1], F32, name="table_load", align_bytes=ALIGN)
        nc.scalar.activation(out=table_load[:], in_=zeros[:, 0:1], func=ACT.Sin)
        ident_bf = keep.tile([P, P], BF16, name="ident_bf", align_bytes=ALIGN)
        nc.scalar.copy(out=ident_bf[:], in_=ident[:])

        warm_up_out = acc_pool.tile([P, P], F32, name="warm_up_out", tag="acc")
        for i in range(WARM_UP):
            nc.tensor.matmul(out=warm_up_out[:], lhsT=zeros[:], rhs=zeros[:], start=True, stop=True)

        bias = keep.tile([P, COLUMN_TILES * COLUMNS], F32, name="bias", align_bytes=ALIGN)
        bias_banks = []
        for n in range(COLUMN_TILES):
            bank = acc_pool.tile([P, COLUMNS], F32, name="bias_bank%d" % n, tag="acc")
            nc.tensor.matmul(
                out=bank[:], lhsT=ident_bf[:, n : n + 1].to_broadcast([P, P]), rhs=bias_rows[:], start=True, stop=True
            )
            bias_banks.append(bank)

        widen(4)
        widen(16)
        flat = angles[:].rearrange("p m j -> p (m j)")
        turns = keep.tile([P, 2, 2 * HALF], I32, name="turns", align_bytes=ALIGN)
        nc.vector.tensor_scalar(out=turns[:, 0, :], in0=flat, scalar1=1.0 / (2.0 * math.pi), scalar2=None, op0=ALU.mult)
        nc.vector.tensor_scalar(
            out=turns[:, 1, :], in0=flat, scalar1=1.0 / (2.0 * math.pi), scalar2=0.25, op0=ALU.mult, op1=ALU.add
        )
        reduced = keep.tile([P, 2, 2 * HALF], F32, name="reduced", align_bytes=ALIGN)
        tables = keep.tile([P, 2, 2, HALF], F32, name="tables", align_bytes=ALIGN)
        tables_psum = tab_pool.tile([P, 2, 2, HALF], F32, name="tables_psum")
        for kind in range(2):
            nc.vector.scalar_tensor_tensor(
                out=reduced[:, kind, :], in0=turns[:, kind, :], scalar=-2.0 * math.pi, in1=flat, op0=ALU.mult, op1=ALU.add
            )
        for kind in range(2):
            nc.scalar.activation(
                out=tables[:, kind, :, :].rearrange("p m j -> p (m j)"),
                in_=reduced[:, kind, :],
                func=ACT.Sin,
                bias=kind * math.pi / 2.0,
            )
            nc.tensor.matmul(
                out=tables_psum[:, kind, :, :].rearrange("p m j -> p (m j)"),
                lhsT=ident[:],
                rhs=tables[:, kind, :, :].rearrange("p m j -> p (m j)"),
                start=True,
                stop=True,
            )
        for n in range(COLUMN_TILES):
            nc.scalar.copy(out=bias[:, n * COLUMNS : (n + 1) * COLUMNS], in_=bias_banks[n][:])

        nc.vector.memset(x_planes[1][:].bitcast(I32), 0)
        for n in range(1, COLUMN_TILES):
            nc.vector.memset(w_planes[n][:].bitcast(I32), 0)
        load_scales(x_planes[1], x_scales, 2 * P, 4 * P)
        load_codes(x23_codes, x_words, 0, PASSES, 512, 1024)
        for n in range(1, COLUMN_TILES):
            c = n % 2
            load_scales(w_planes[n], w_scales[n // 2], c * COLUMNS, (c + 1) * COLUMNS)
            load_codes(w_codes[n], w_words[n // 2], 0, PASSES, c * 2 * COLUMNS, (c + 1) * 2 * COLUMNS)

        units = [(n, m, 0, COLUMNS) for n in range(COLUMN_TILES) for m in range(TOKEN_TILES)]
        units = units[:-1] + [(COLUMN_TILES - 1, TOKEN_TILES - 1, c0, COLUMNS // 2) for c0 in (0, COLUMNS // 2)]
        last = len(units) - 1
        z_of = {}
        block_of = {}

        def block(k):
            paired = k < PAIRED_UNITS
            key = k // 2 if paired else k
            if key not in block_of:
                width = 2 * COLUMNS if paired else units[k][3]
                suffix = "2" if paired else "1"
                block_of[key] = [
                    work.tile([P, width], F32, name=nm + suffix, tag=nm + suffix, bufs=5, align_bytes=ALIGN)
                    for nm in ("zc", "zs", "res")
                ]
            return block_of[key], (k % 2) * COLUMNS if paired else 0

        def project(k):
            n, m, c0, w = units[k]
            acc = acc_pool.tile([P, w], F32, name="acc", tag="acc")
            for g in range(PASSES):
                nc.tensor.matmul_mx(
                    out=acc[:],
                    lhsT=stationary_codes(m, g).bitcast(FP4X4),
                    lhsT_scale=stationary_scales(m, g),
                    rhs=moving_codes(n, g)[:, 2 * c0 : 2 * (c0 + w)].bitcast(FP4X4),
                    rhs_scale=w_planes[n][:, g, c0 : c0 + w],
                    start=(g == 0),
                    stop=(g == PASSES - 1),
                )
            z = work.tile([P, w], F32, name="z", tag="z", bufs=6, align_bytes=ALIGN)
            nc.vector.tensor_tensor(out=z[:], in0=acc[:], in1=bias[:, n * COLUMNS + c0 : n * COLUMNS + c0 + w], op=ALU.add)
            z_of[k] = z

        def times_cosine(k):
            n, m, c0, w = units[k]
            tiles, b0 = block(k)
            on_gpsimd = k in GPSIMD_COSINE_UNITS
            engine = nc.gpsimd if on_gpsimd else nc.vector
            table = tables if on_gpsimd else tables_psum
            engine.tensor_tensor(
                out=tiles[0][:, b0 : b0 + w].rearrange("p (c j) -> p c j", j=HALF),
                in0=z_of[k][:].rearrange("p (c j) -> p c j", j=HALF),
                in1=table[:, 1, m % 2, :].unsqueeze(1).to_broadcast([P, w // HALF, HALF]),
                op=ALU.mult,
            )

        def times_sine(k):
            n, m, c0, w = units[k]
            tiles, b0 = block(k)
            nc.vector.tensor_tensor(
                out=tiles[1][:, b0 : b0 + w].rearrange("p (c i t) -> p c i t", i=HALF // 2, t=2),
                in0=z_of[k][:].rearrange("p (c i t) -> p c i t", i=HALF // 2, t=2)[:, :, :, ::-1],
                in1=tables_psum[:, 0, m % 2, :]
                .rearrange("p (i t) -> p i t", t=2)
                .unsqueeze(1)
                .to_broadcast([P, w // HALF, HALF // 2, 2]),
                op=ALU.mult,
            )

        def finish(ks, engine):
            tiles, b0 = block(ks[0])
            engine.tensor_tensor(out=tiles[2][:], in0=tiles[0][:], in1=tiles[1][:], op=ALU.add)
            for k in ks:
                n, m, c0, w = units[k]
                tiles, b0 = block(k)
                h0 = (n % 2) * 4 + c0 // HEAD
                pos0 = (m % 2) * P
                queue = nc.sync if k == last else nc.scalar
                queue.dma_start(
                    out=outs[n // 2][m // 2, h0 : h0 + w // HEAD, pos0 : pos0 + P, :].rearrange("h p d -> p h d"),
                    in_=tiles[2][:, b0 : b0 + w].rearrange("p (h d) -> p h d", d=HEAD),
                )

        for k in range(len(units)):
            project(k)
            if k > 0:
                times_sine(k - 1)
            times_cosine(k)
            if k > 0:
                if k - 1 >= PAIRED_UNITS:
                    finish([k - 1], nc.gpsimd)
                elif (k - 1) % 2 == 1:
                    finish([k - 2, k - 1], nc.gpsimd)
        times_sine(last)
        finish([last], nc.vector)
